import numpy as np
import ml_dtypes


def mxq(x, axis, fmt="e4m3"):
    dtype, down = {"e4m3": (ml_dtypes.float8_e4m3fn, 7), "e5m2": (ml_dtypes.float8_e5m2, 14)}[fmt]
    v = np.moveaxis(np.asarray(x, np.float32).astype(ml_dtypes.bfloat16).astype(np.float64), axis, -1)
    blocks = v.reshape(v.shape[:-1] + (-1, 32))
    amax = np.abs(blocks).max(-1, keepdims=True)
    byte = np.maximum(np.where(amax > 0, np.frexp(amax)[1] - 1 + 127, 0) - down, 1)
    scale = np.exp2(byte - 127.0)
    codes = (blocks / scale).astype(np.float32).astype(dtype).astype(np.float64)
    return np.moveaxis((codes * scale).reshape(v.shape), -1, axis)


WIDE = False


def mx_kscale(k):
    if not WIDE:
        return np.ones(k)
    levels = np.array([10, -10, 5, -5, 0])
    a = np.random.permutation(np.resize(levels, k // 512 * 4)).reshape(k // 512, 4)
    idx = np.arange(k)
    return np.exp2(a[idx // 512, idx % 128 // 32])


BF16 = ml_dtypes.bfloat16


def bf(x):
    return np.asarray(x, np.float32).astype(BF16)


def f64(x):
    return np.asarray(x).astype(np.float64)


B, HW, C, HID, WS, SS, HEADS = 1, 32, 1024, 2048, 8, 4, 16
L = HW * HW
NH = HW // WS
EPS = 1e-5


def adain(x, scale, shift):
    m = x.mean(2, keepdims=True)
    s = np.std(x, axis=2, keepdims=True, ddof=1) + EPS
    return (x - m) / s * scale + shift


def setup_inputs():
    s = mx_kscale(C)
    return {"o_attn": bf(0.4 * np.random.standard_normal((NH * NH * B, WS * WS, C)) * s),
            "out_w": bf(np.random.standard_normal((C, C)) / np.sqrt(C) / s[None, :]),
            "out_b": bf(0.1 * np.random.standard_normal(C)),
            "ada1_scale": bf(1.0 + 0.1 * np.random.standard_normal((1, L, 1))),
            "ada1_shift": bf(0.1 * np.random.standard_normal((1, L, 1))),
            "x": bf(np.random.standard_normal((B, L, C)))}


def reference(o_attn, out_w, out_b, ada1_scale, ada1_shift, x):
    a = (mxq(f64(o_attn), 2, "e4m3") @ mxq(f64(out_w), 1, "e4m3").T) + f64(out_b)
    a = np.swapaxes(a.reshape(B, NH, NH, WS, WS, C), 2, 3).reshape(B, HW, HW, C)
    a = np.roll(a, (SS, SS), axis=(1, 2)).reshape(B, L, C)
    return f64(x) + adain(a, f64(ada1_scale), f64(ada1_shift))

@@ -1,0 +1,307 @@
+from contextlib import ExitStack
+
+import concourse.mybir as mybir
+from concourse.masks import make_identity
+
+F32 = mybir.dt.float32
+BF16 = mybir.dt.bfloat16
+U32 = mybir.dt.uint32
+U8 = mybir.dt.uint8
+FP8X4 = mybir.dt.float8_e4m3fn_x4
+ALU = mybir.AluOpType
+ACT = mybir.ActivationFunctionType
+
+P = 128
+TOKENS = 1024
+CHANNELS = 1024
+K = 1024
+K_PASS = 4 * P
+PASSES = K // K_PASS
+N_TILE = 512
+N_TILES = CHANNELS // N_TILE
+TOKEN_TILES = TOKENS // P
+GRID = 32
+WINDOW = 8
+SHIFT = 4
+PAIR = 2
+GROUPS = TOKEN_TILES // PAIR
+EPS = 1e-5
+
+FLOPS = 2 * TOKENS * CHANNELS * K
+
+
+def transpose_block(nc, psum, words, order):
+    turned = psum.tile([P, PASSES, 2, P], F32, name="turned")
+    for g in range(PASSES):
+        for u in range(2):
+            first = (2 * g + u) * P
+            nc.tensor.transpose(turned[:, g, u, :], words[:, first : first + P], order)
+    return turned
+
+
+def quantise(nc, grouped, codes, scales, columns):
+    for g in range(PASSES):
+        nc.vector.quantize_mx(
+            out=codes[:, g, columns].bitcast(FP8X4),
+            scales=scales[:, g, columns],
+            in_=grouped[:, g, columns, :].rearrange("p c t -> p (c t)"),
+        )
+
+
+def tile_swintransformerblock_pb_kernel(
+    tc, o_attn, out_w, out_b, ada1_scale, ada1_shift, x, out
+):
+    nc = tc.nc
+    attn_rows = o_attn.flatten_outer_dims()
+    x_rows = x.flatten_outer_dims()
+    out_rows = out.flatten_outer_dims()
+
+    with ExitStack() as stack:
+        const = stack.enter_context(tc.tile_pool(name="const", bufs=1))
+        keep = stack.enter_context(tc.tile_pool(name="keep", bufs=1))
+        work = stack.enter_context(tc.tile_pool(name="work", bufs=4))
+        psum_turned = stack.enter_context(tc.psum_pool(name="psum_turned", bufs=4))
+        psum_acc = stack.enter_context(tc.psum_pool(name="psum_acc", bufs=4))
+        stack.enter_context(tc.manual_schedule())
+
+        bias_row = const.tile([P, CHANNELS], BF16)
+        nc.vector.memset(bias_row[:], 0.0)
+        ada_rows = const.tile([P, P], BF16)
+        nc.vector.memset(ada_rows[:], 0.0)
+        nc.scalar.dma_start(out=bias_row[0:1, :], in_=out_b.unsqueeze(0))
+        for first, vector in ((0, ada1_scale), (TOKEN_TILES, ada1_shift)):
+            rows = vector.rearrange("o (t p) i -> (o t) (p i)", p=P)
+            nc.scalar.dma_start(
+                out=ada_rows[first : first + TOKEN_TILES - 1, :], in_=rows[1:TOKEN_TILES, :]
+            )
+            nc.scalar.dma_start(
+                out=ada_rows[first + TOKEN_TILES - 1 : first + TOKEN_TILES, :], in_=rows[0:1, :]
+            )
+
+        warm = const.tile([P, 1], F32)
+        nc.vector.memset(warm[:], 1.0)
+        nc.scalar.activation(out=warm[:], in_=warm[:], func=ACT.Sqrt)
+        ones = const.tile([P, P], BF16)
+        nc.vector.memset(ones[:], 1.0)
+
+        identity = const.tile([P, P], F32)
+        make_identity(nc, identity[:])
+        identity_bf16 = const.tile([P, P], BF16)
+        nc.vector.tensor_copy(out=identity_bf16[:], in_=identity[:])
+
+        order_left = const.tile([P, P], F32)
+        nc.vector.tensor_copy(
+            out=order_left[:].rearrange("p (r d c) -> p r d c", r=WINDOW, d=2),
+            in_=identity[:].rearrange("p (d r c) -> p r d c", d=2, r=WINDOW),
+        )
+        stay = 2 * WINDOW - SHIFT
+        order_right = const.tile([P, P], F32)
+        staying = order_right[:, 0 : WINDOW * stay].rearrange("p (r j) -> p r j", j=stay)
+        wrapping = order_right[:, WINDOW * stay : P].rearrange("p (r j) -> p r j", j=SHIFT)
+        window2 = identity[:, 0:64].rearrange("p (r c) -> p r c", c=WINDOW)
+        window3 = identity[:, 64:128].rearrange("p (r c) -> p r c", c=WINDOW)
+        nc.vector.tensor_copy(out=staying[:, :, 0:WINDOW], in_=window2)
+        nc.vector.tensor_copy(out=staying[:, :, WINDOW:stay], in_=window3[:, :, 0 : WINDOW - SHIFT])
+        nc.vector.tensor_copy(out=wrapping, in_=window3[:, :, WINDOW - SHIFT : WINDOW])
+
+        w_raw = keep.tile([P, TOKEN_TILES, K], BF16)
+        a_raw = keep.tile([P, TOKEN_TILES, K], BF16)
+        x_sb = keep.tile([P, TOKEN_TILES, CHANNELS], BF16)
+
+        def load_pair(raw, rows, pair):
+            blocks = slice(PAIR * pair, PAIR * pair + PAIR)
+            nc.sync.dma_start(
+                out=raw[:, blocks, :],
+                in_=rows[PAIR * P * pair : PAIR * P * (pair + 1), :].rearrange(
+                    "(b p) k -> p b k", p=P
+                ),
+            )
+
+        def output_rows(tau):
+            first = ((tau + 1) % TOKEN_TILES) * P
+            return slice(first, first + P)
+
+        def load_x(group):
+            for tau in range(PAIR * group, PAIR * group + PAIR):
+                nc.sync.dma_start(out=x_sb[:, tau, :], in_=x_rows[output_rows(tau), :])
+
+        load_pair(w_raw, out_w, 0)
+        load_pair(w_raw, out_w, 1)
+        load_pair(a_raw, attn_rows, 0)
+        load_pair(w_raw, out_w, 2)
+        load_pair(w_raw, out_w, 3)
+        load_pair(a_raw, attn_rows, 1)
+        load_pair(a_raw, attn_rows, 2)
+        load_x(0)
+        load_pair(a_raw, attn_rows, 3)
+        for group in range(1, GROUPS):
+            load_x(group)
+
+        w_grouped = keep.tile([P, PASSES, CHANNELS, 4], BF16, align_bytes=64)
+        w_codes = keep.tile([P, PASSES, CHANNELS], U32, align_bytes=64)
+        w_scales = keep.tile([P, PASSES, CHANNELS], U8, align_bytes=64)
+        a_grouped = keep.tile([P, PASSES, TOKENS, 4], BF16, align_bytes=64)
+        a_codes = keep.tile([P, PASSES, TOKENS], U32, align_bytes=64)
+        a_scales = keep.tile([P, PASSES, TOKENS], U8, align_bytes=64)
+        w_words = w_grouped[:].bitcast(F32)
+        a_grid = a_grouped[:].bitcast(F32).rearrange("p g (i j) u -> p g i j u", j=GRID)
+
+        def prepare_weights(pair):
+            for block in range(PAIR * pair, PAIR * pair + PAIR):
+                turned = transpose_block(
+                    nc, psum_turned, w_raw[:, block, :].bitcast(F32), identity[:]
+                )
+                target = w_words[:, :, block * P : (block + 1) * P, :]
+                source = turned[:].rearrange("p g u c -> p g c u")
+                if block % 2 == 0:
+                    nc.vector.tensor_copy(out=target, in_=source)
+                else:
+                    nc.scalar.copy(out=target, in_=source)
+            quantise(nc, w_grouped, w_codes, w_scales, slice(PAIR * P * pair, PAIR * P * (pair + 1)))
+
+        def prepare_tokens(group):
+            grid_rows = slice(WINDOW * group, WINDOW * (group + 1))
+            left = transpose_block(
+                nc, psum_turned, a_raw[:, PAIR * group, :].bitcast(F32), order_left[:]
+            )
+            nc.scalar.copy(
+                out=a_grid[:, :, grid_rows, SHIFT : SHIFT + 2 * WINDOW, :],
+                in_=left[:].rearrange("p g u (r j) -> p g r j u", j=2 * WINDOW),
+            )
+            right = transpose_block(
+                nc, psum_turned, a_raw[:, PAIR * group + 1, :].bitcast(F32), order_right[:]
+            )
+            nc.scalar.copy(
+                out=a_grid[:, :, grid_rows, GRID - stay : GRID, :],
+                in_=right[:, :, :, 0 : WINDOW * stay].rearrange("p g u (r j) -> p g r j u", j=stay),
+            )
+            nc.scalar.copy(
+                out=a_grid[:, :, grid_rows, 0:SHIFT, :],
+                in_=right[:, :, :, WINDOW * stay : P].rearrange("p g u (r j) -> p g r j u", j=SHIFT),
+            )
+            quantise(nc, a_grouped, a_codes, a_scales, slice(PAIR * P * group, PAIR * P * (group + 1)))
+
+        bias_all = const.tile([P, CHANNELS], F32)
+        ada = const.tile([P, 2 * TOKEN_TILES], F32)
+        ada_gain = ada[:, 0:TOKEN_TILES]
+        ada_offset = ada[:, TOKEN_TILES : 2 * TOKEN_TILES]
+
+        def spread_small_vectors():
+            for n in range(N_TILES):
+                columns = slice(n * N_TILE, (n + 1) * N_TILE)
+                spread = psum_acc.tile([P, N_TILE], F32, name="acc")
+                nc.tensor.matmul(
+                    out=spread[:], lhsT=ones[:], rhs=bias_row[:, columns], start=True, stop=True
+                )
+                nc.scalar.copy(out=bias_all[:, columns], in_=spread[:])
+            ada_turned = psum_turned.tile([P, P], BF16, name="turned")
+            nc.tensor.transpose(ada_turned[:], ada_rows[:], identity_bf16[:])
+            nc.vector.tensor_copy(out=ada[:], in_=ada_turned[:, 0 : 2 * TOKEN_TILES])
+
+        sums = const.tile([P, TOKEN_TILES, N_TILES], F32)
+        scaled_sums = const.tile([P, TOKEN_TILES, N_TILES], F32)
+        minus_mean = const.tile([P, TOKEN_TILES], F32)
+        squares = const.tile([P, TOKEN_TILES], F32)
+        std = const.tile([P, TOKEN_TILES], F32)
+        inv_std = const.tile([P, TOKEN_TILES], F32)
+        gain = const.tile([P, TOKEN_TILES], F32)
+        offset = const.tile([P, TOKEN_TILES], F32)
+        projected = {}
+        result = {}
+
+        def project(group):
+            taus = range(PAIR * group, PAIR * group + PAIR)
+            pair = slice(PAIR * group, PAIR * group + PAIR)
+            for tau in taus:
+                projected[tau] = work.tile([P, CHANNELS], F32, name="projected")
+            for n in range(N_TILES):
+                columns = slice(n * N_TILE, (n + 1) * N_TILE)
+                for tau in taus:
+                    tokens = slice(tau * P, (tau + 1) * P)
+                    acc = psum_acc.tile([P, N_TILE], F32, name="acc")
+                    for g in range(PASSES):
+                        nc.tensor.matmul_mx(
+                            out=acc[:],
+                            lhsT=a_codes[:, g, tokens].bitcast(FP8X4),
+                            lhsT_scale=a_scales[:, g, tokens],
+                            rhs=w_codes[:, g, columns].bitcast(FP8X4),
+                            rhs_scale=w_scales[:, g, columns],
+                            start=(g == 0),
+                            stop=(g == PASSES - 1),
+                        )
+                    nc.vector.scalar_tensor_tensor(
+                        out=projected[tau][:, columns],
+                        in0=acc[:],
+                        scalar=1.0,
+                        in1=bias_all[:, columns],
+                        op0=ALU.mult,
+                        op1=ALU.add,
+                        accum_out=sums[:, tau, n : n + 1],
+                    )
+            for tau in taus:
+                nc.scalar.activation(
+                    out=scaled_sums[:, tau, :],
+                    in_=sums[:, tau, :],
+                    func=ACT.Identity,
+                    scale=-1.0 / CHANNELS,
+                    accum_out=minus_mean[:, tau : tau + 1],
+                )
+                deviation_squared = work.tile([P, CHANNELS], BF16, name="deviation_squared")
+                nc.scalar.activation(
+                    out=deviation_squared[:],
+                    in_=projected[tau][:],
+                    func=ACT.Square,
+                    bias=minus_mean[:, tau : tau + 1],
+                    accum_out=squares[:, tau : tau + 1],
+                )
+            nc.scalar.activation(
+                out=std[:, pair], in_=squares[:, pair], func=ACT.Sqrt, scale=1.0 / (CHANNELS - 1)
+            )
+
+        def shift_residual(group):
+            pair = slice(PAIR * group, PAIR * group + PAIR)
+            nc.vector.tensor_scalar_add(out=inv_std[:, pair], in0=std[:, pair], scalar1=EPS)
+            nc.vector.reciprocal(out=inv_std[:, pair], in_=inv_std[:, pair])
+            nc.vector.tensor_mul(out=gain[:, pair], in0=inv_std[:, pair], in1=ada_gain[:, pair])
+            nc.vector.tensor_mul(out=offset[:, pair], in0=minus_mean[:, pair], in1=gain[:, pair])
+            nc.vector.tensor_add(out=offset[:, pair], in0=offset[:, pair], in1=ada_offset[:, pair])
+            for tau in range(PAIR * group, PAIR * group + PAIR):
+                result[tau] = work.tile([P, CHANNELS], F32, name="result")
+                nc.gpsimd.tensor_scalar(
+                    out=result[tau][:],
+                    in0=x_sb[:, tau, :],
+                    scalar1=1.0,
+                    scalar2=offset[:, tau : tau + 1],
+                    op0=ALU.mult,
+                    op1=ALU.add,
+                )
+
+        def finish(group):
+            for tau in range(PAIR * group, PAIR * group + PAIR):
+                nc.vector.scalar_tensor_tensor(
+                    out=result[tau][:],
+                    in0=projected[tau][:],
+                    scalar=gain[:, tau : tau + 1],
+                    in1=result[tau][:],
+                    op0=ALU.mult,
+                    op1=ALU.add,
+                )
+                nc.sync.dma_start(out=out_rows[output_rows(tau), :], in_=result[tau][:])
+
+        prepare_weights(0)
+        prepare_weights(1)
+        prepare_tokens(0)
+        spread_small_vectors()
+        prepare_weights(2)
+        prepare_weights(3)
+        prepare_tokens(1)
+        for group in range(GROUPS):
+            if group > 0:
+                shift_residual(group - 1)
+            project(group)
+            if group > 0:
+                finish(group - 1)
+            if group + 2 < GROUPS:
+                prepare_tokens(group + 2)
+        shift_residual(GROUPS - 1)
+        finish(GROUPS - 1)

@@ -59,7 +59,7 @@ def tile_swintransformerblock_pb_kernel(
     with ExitStack() as stack:
         const = stack.enter_context(tc.tile_pool(name="const", bufs=1))
         keep = stack.enter_context(tc.tile_pool(name="keep", bufs=1))
-        work = stack.enter_context(tc.tile_pool(name="work", bufs=4))
+        work = stack.enter_context(tc.tile_pool(name="work", bufs=TOKEN_TILES))
         psum_turned = stack.enter_context(tc.psum_pool(name="psum_turned", bufs=4))
         psum_acc = stack.enter_context(tc.psum_pool(name="psum_acc", bufs=4))
         stack.enter_context(tc.manual_schedule())
@@ -125,16 +125,12 @@ def tile_swintransformerblock_pb_kernel(
             for tau in range(PAIR * group, PAIR * group + PAIR):
                 nc.sync.dma_start(out=x_sb[:, tau, :], in_=x_rows[output_rows(tau), :])
 
-        load_pair(w_raw, out_w, 0)
-        load_pair(w_raw, out_w, 1)
         load_pair(a_raw, attn_rows, 0)
-        load_pair(w_raw, out_w, 2)
-        load_pair(w_raw, out_w, 3)
-        load_pair(a_raw, attn_rows, 1)
-        load_pair(a_raw, attn_rows, 2)
-        load_x(0)
-        load_pair(a_raw, attn_rows, 3)
+        for pair in range(GROUPS):
+            load_pair(w_raw, out_w, pair)
         for group in range(1, GROUPS):
+            load_pair(a_raw, attn_rows, group)
+        for group in range(GROUPS):
             load_x(group)
 
         w_grouped = keep.tile([P, PASSES, CHANNELS, 4], BF16, align_bytes=64)
@@ -146,20 +142,20 @@ def tile_swintransformerblock_pb_kernel(
         w_words = w_grouped[:].bitcast(F32)
         a_grid = a_grouped[:].bitcast(F32).rearrange("p g (i j) u -> p g i j u", j=GRID)
 
-        def prepare_weights(pair):
+        def turn_weights(pair):
             for block in range(PAIR * pair, PAIR * pair + PAIR):
                 turned = transpose_block(
                     nc, psum_turned, w_raw[:, block, :].bitcast(F32), identity[:]
                 )
-                target = w_words[:, :, block * P : (block + 1) * P, :]
-                source = turned[:].rearrange("p g u c -> p g c u")
-                if block % 2 == 0:
-                    nc.vector.tensor_copy(out=target, in_=source)
-                else:
-                    nc.scalar.copy(out=target, in_=source)
+                nc.scalar.copy(
+                    out=w_words[:, :, block * P : (block + 1) * P, :],
+                    in_=turned[:].rearrange("p g u c -> p g c u"),
+                )
+
+        def quantise_weights(pair):
             quantise(nc, w_grouped, w_codes, w_scales, slice(PAIR * P * pair, PAIR * P * (pair + 1)))
 
-        def prepare_tokens(group):
+        def turn_tokens(group):
             grid_rows = slice(WINDOW * group, WINDOW * (group + 1))
             left = transpose_block(
                 nc, psum_turned, a_raw[:, PAIR * group, :].bitcast(F32), order_left[:]
@@ -179,12 +175,15 @@ def tile_swintransformerblock_pb_kernel(
                 out=a_grid[:, :, grid_rows, 0:SHIFT, :],
                 in_=right[:, :, :, WINDOW * stay : P].rearrange("p g u (r j) -> p g r j u", j=SHIFT),
             )
+
+        def quantise_tokens(group):
             quantise(nc, a_grouped, a_codes, a_scales, slice(PAIR * P * group, PAIR * P * (group + 1)))
 
         bias_all = const.tile([P, CHANNELS], F32)
         ada = const.tile([P, 2 * TOKEN_TILES], F32)
         ada_gain = ada[:, 0:TOKEN_TILES]
         ada_offset = ada[:, TOKEN_TILES : 2 * TOKEN_TILES]
+        inv_ada_gain = const.tile([P, TOKEN_TILES], F32)
 
         def spread_small_vectors():
             for n in range(N_TILES):
@@ -193,17 +192,17 @@ def tile_swintransformerblock_pb_kernel(
                 nc.tensor.matmul(
                     out=spread[:], lhsT=ones[:], rhs=bias_row[:, columns], start=True, stop=True
                 )
-                nc.scalar.copy(out=bias_all[:, columns], in_=spread[:])
+                nc.vector.tensor_copy(out=bias_all[:, columns], in_=spread[:])
             ada_turned = psum_turned.tile([P, P], BF16, name="turned")
             nc.tensor.transpose(ada_turned[:], ada_rows[:], identity_bf16[:])
             nc.vector.tensor_copy(out=ada[:], in_=ada_turned[:, 0 : 2 * TOKEN_TILES])
+            nc.vector.reciprocal(out=inv_ada_gain[:], in_=ada_gain)
 
         sums = const.tile([P, TOKEN_TILES, N_TILES], F32)
         scaled_sums = const.tile([P, TOKEN_TILES, N_TILES], F32)
         minus_mean = const.tile([P, TOKEN_TILES], F32)
         squares = const.tile([P, TOKEN_TILES], F32)
         std = const.tile([P, TOKEN_TILES], F32)
-        inv_std = const.tile([P, TOKEN_TILES], F32)
         gain = const.tile([P, TOKEN_TILES], F32)
         offset = const.tile([P, TOKEN_TILES], F32)
         projected = {}
@@ -212,16 +211,15 @@ def tile_swintransformerblock_pb_kernel(
         def project(group):
             taus = range(PAIR * group, PAIR * group + PAIR)
             pair = slice(PAIR * group, PAIR * group + PAIR)
-            for tau in taus:
-                projected[tau] = work.tile([P, CHANNELS], F32, name="projected")
+            acc = {}
             for n in range(N_TILES):
                 columns = slice(n * N_TILE, (n + 1) * N_TILE)
                 for tau in taus:
                     tokens = slice(tau * P, (tau + 1) * P)
-                    acc = psum_acc.tile([P, N_TILE], F32, name="acc")
+                    acc[tau, n] = psum_acc.tile([P, N_TILE], F32, name="acc")
                     for g in range(PASSES):
                         nc.tensor.matmul_mx(
-                            out=acc[:],
+                            out=acc[tau, n][:],
                             lhsT=a_codes[:, g, tokens].bitcast(FP8X4),
                             lhsT_scale=a_scales[:, g, tokens],
                             rhs=w_codes[:, g, columns].bitcast(FP8X4),
@@ -229,9 +227,16 @@ def tile_swintransformerblock_pb_kernel(
                             start=(g == 0),
                             stop=(g == PASSES - 1),
                         )
+            if group + 3 < GROUPS:
+                turn_tokens(group + 3)
+            for tau in taus:
+                projected[tau] = work.tile([P, CHANNELS], F32, name="projected")
+            for n in range(N_TILES):
+                columns = slice(n * N_TILE, (n + 1) * N_TILE)
+                for tau in taus:
                     nc.vector.scalar_tensor_tensor(
                         out=projected[tau][:, columns],
-                        in0=acc[:],
+                        in0=acc[tau, n][:],
                         scalar=1.0,
                         in1=bias_all[:, columns],
                         op0=ALU.mult,
@@ -260,21 +265,42 @@ def tile_swintransformerblock_pb_kernel(
 
         def shift_residual(group):
             pair = slice(PAIR * group, PAIR * group + PAIR)
-            nc.vector.tensor_scalar_add(out=inv_std[:, pair], in0=std[:, pair], scalar1=EPS)
-            nc.vector.reciprocal(out=inv_std[:, pair], in_=inv_std[:, pair])
-            nc.vector.tensor_mul(out=gain[:, pair], in0=inv_std[:, pair], in1=ada_gain[:, pair])
-            nc.vector.tensor_mul(out=offset[:, pair], in0=minus_mean[:, pair], in1=gain[:, pair])
-            nc.vector.tensor_add(out=offset[:, pair], in0=offset[:, pair], in1=ada_offset[:, pair])
+            nc.vector.scalar_tensor_tensor(
+                out=gain[:, pair],
+                in0=std[:, pair],
+                scalar=EPS,
+                in1=inv_ada_gain[:, pair],
+                op0=ALU.add,
+                op1=ALU.mult,
+            )
+            nc.vector.reciprocal(out=gain[:, pair], in_=gain[:, pair])
             for tau in range(PAIR * group, PAIR * group + PAIR):
-                result[tau] = work.tile([P, CHANNELS], F32, name="result")
-                nc.gpsimd.tensor_scalar(
-                    out=result[tau][:],
-                    in0=x_sb[:, tau, :],
-                    scalar1=1.0,
-                    scalar2=offset[:, tau : tau + 1],
+                nc.vector.tensor_scalar(
+                    out=offset[:, tau : tau + 1],
+                    in0=minus_mean[:, tau : tau + 1],
+                    scalar1=gain[:, tau : tau + 1],
+                    scalar2=ada_offset[:, tau : tau + 1],
                     op0=ALU.mult,
                     op1=ALU.add,
                 )
+            for tau in range(PAIR * group, PAIR * group + PAIR):
+                result[tau] = work.tile([P, CHANNELS], F32, name="result")
+                if tau < TOKEN_TILES // 2:
+                    nc.gpsimd.tensor_scalar(
+                        out=result[tau][:],
+                        in0=x_sb[:, tau, :],
+                        scalar1=1.0,
+                        scalar2=offset[:, tau : tau + 1],
+                        op0=ALU.mult,
+                        op1=ALU.add,
+                    )
+                else:
+                    nc.scalar.activation(
+                        out=result[tau][:],
+                        in_=x_sb[:, tau, :],
+                        func=ACT.Identity,
+                        bias=offset[:, tau : tau + 1],
+                    )
 
         def finish(group):
             for tau in range(PAIR * group, PAIR * group + PAIR):
@@ -288,20 +314,23 @@ def tile_swintransformerblock_pb_kernel(
                 )
                 nc.sync.dma_start(out=out_rows[output_rows(tau), :], in_=result[tau][:])
 
-        prepare_weights(0)
-        prepare_weights(1)
-        prepare_tokens(0)
+        turn_tokens(0)
+        quantise_tokens(0)
+        turn_weights(0)
         spread_small_vectors()
-        prepare_weights(2)
-        prepare_weights(3)
-        prepare_tokens(1)
-        for group in range(GROUPS):
-            if group > 0:
-                shift_residual(group - 1)
-            project(group)
-            if group > 0:
-                finish(group - 1)
-            if group + 2 < GROUPS:
-                prepare_tokens(group + 2)
-        shift_residual(GROUPS - 1)
-        finish(GROUPS - 1)
+        quantise_weights(0)
+        for pair in range(1, GROUPS):
+            turn_weights(pair)
+            quantise_weights(pair)
+        turn_tokens(1)
+        turn_tokens(2)
+        quantise_tokens(1)
+        for step in range(GROUPS + 3):
+            if step < GROUPS:
+                project(step)
+            if step + 2 < GROUPS:
+                quantise_tokens(step + 2)
+            if step >= 3:
+                finish(step - 3)
+            if 1 <= step <= GROUPS:
+                shift_residual(step - 1)

@@ -20,6 +20,7 @@ PASSES = K // K_PASS
 N_TILE = 512
 N_TILES = CHANNELS // N_TILE
 TOKEN_TILES = TOKENS // P
+W_BLOCKS = CHANNELS // P
 GRID = 32
 WINDOW = 8
 SHIFT = 4
@@ -104,15 +105,15 @@ def tile_swintransformerblock_pb_kernel(
         nc.vector.tensor_copy(out=staying[:, :, WINDOW:stay], in_=window3[:, :, 0 : WINDOW - SHIFT])
         nc.vector.tensor_copy(out=wrapping, in_=window3[:, :, WINDOW - SHIFT : WINDOW])
 
-        w_raw = keep.tile([P, TOKEN_TILES, K], BF16)
+        w_raw = keep.tile([P, W_BLOCKS, K], BF16)
         a_raw = keep.tile([P, TOKEN_TILES, K], BF16)
         x_sb = keep.tile([P, TOKEN_TILES, CHANNELS], BF16)
 
-        def load_pair(raw, rows, pair):
-            blocks = slice(PAIR * pair, PAIR * pair + PAIR)
+        def load_tokens(group):
+            blocks = slice(PAIR * group, PAIR * group + PAIR)
             nc.sync.dma_start(
-                out=raw[:, blocks, :],
-                in_=rows[PAIR * P * pair : PAIR * P * (pair + 1), :].rearrange(
+                out=a_raw[:, blocks, :],
+                in_=attn_rows[PAIR * P * group : PAIR * P * (group + 1), :].rearrange(
                     "(b p) k -> p b k", p=P
                 ),
             )
@@ -125,11 +126,11 @@ def tile_swintransformerblock_pb_kernel(
             for tau in range(PAIR * group, PAIR * group + PAIR):
                 nc.sync.dma_start(out=x_sb[:, tau, :], in_=x_rows[output_rows(tau), :])
 
-        load_pair(a_raw, attn_rows, 0)
-        for pair in range(GROUPS):
-            load_pair(w_raw, out_w, pair)
+        load_tokens(0)
+        for block in range(W_BLOCKS):
+            nc.sync.dma_start(out=w_raw[:, block, :], in_=out_w[block * P : (block + 1) * P, :])
         for group in range(1, GROUPS):
-            load_pair(a_raw, attn_rows, group)
+            load_tokens(group)
         for group in range(GROUPS):
             load_x(group)
 
@@ -142,18 +143,13 @@ def tile_swintransformerblock_pb_kernel(
         w_words = w_grouped[:].bitcast(F32)
         a_grid = a_grouped[:].bitcast(F32).rearrange("p g (i j) u -> p g i j u", j=GRID)
 
-        def turn_weights(pair):
-            for block in range(PAIR * pair, PAIR * pair + PAIR):
-                turned = transpose_block(
-                    nc, psum_turned, w_raw[:, block, :].bitcast(F32), identity[:]
-                )
-                nc.scalar.copy(
-                    out=w_words[:, :, block * P : (block + 1) * P, :],
-                    in_=turned[:].rearrange("p g u c -> p g c u"),
-                )
-
-        def quantise_weights(pair):
-            quantise(nc, w_grouped, w_codes, w_scales, slice(PAIR * P * pair, PAIR * P * (pair + 1)))
+        def prepare_weights(block):
+            rows = slice(block * P, (block + 1) * P)
+            turned = transpose_block(nc, psum_turned, w_raw[:, block, :].bitcast(F32), identity[:])
+            nc.scalar.copy(
+                out=w_words[:, :, rows, :], in_=turned[:].rearrange("p g u c -> p g c u")
+            )
+            quantise(nc, w_grouped, w_codes, w_scales, rows)
 
         def turn_tokens(group):
             grid_rows = slice(WINDOW * group, WINDOW * (group + 1))
@@ -199,12 +195,11 @@ def tile_swintransformerblock_pb_kernel(
             nc.vector.reciprocal(out=inv_ada_gain[:], in_=ada_gain)
 
         sums = const.tile([P, TOKEN_TILES, N_TILES], F32)
-        scaled_sums = const.tile([P, TOKEN_TILES, N_TILES], F32)
         minus_mean = const.tile([P, TOKEN_TILES], F32)
         squares = const.tile([P, TOKEN_TILES], F32)
         std = const.tile([P, TOKEN_TILES], F32)
         gain = const.tile([P, TOKEN_TILES], F32)
-        offset = const.tile([P, TOKEN_TILES], F32)
+        offset = {}
         projected = {}
         result = {}
 
@@ -244,12 +239,13 @@ def tile_swintransformerblock_pb_kernel(
                         accum_out=sums[:, tau, n : n + 1],
                     )
             for tau in taus:
-                nc.scalar.activation(
-                    out=scaled_sums[:, tau, :],
-                    in_=sums[:, tau, :],
-                    func=ACT.Identity,
-                    scale=-1.0 / CHANNELS,
-                    accum_out=minus_mean[:, tau : tau + 1],
+                nc.gpsimd.tensor_scalar(
+                    out=minus_mean[:, tau : tau + 1],
+                    in0=sums[:, tau, 0:1],
+                    scalar1=sums[:, tau, 1:2],
+                    scalar2=-1.0 / CHANNELS,
+                    op0=ALU.add,
+                    op1=ALU.mult,
                 )
                 deviation_squared = work.tile([P, CHANNELS], BF16, name="deviation_squared")
                 nc.scalar.activation(
@@ -275,53 +271,64 @@ def tile_swintransformerblock_pb_kernel(
             )
             nc.vector.reciprocal(out=gain[:, pair], in_=gain[:, pair])
             for tau in range(PAIR * group, PAIR * group + PAIR):
-                nc.vector.tensor_scalar(
-                    out=offset[:, tau : tau + 1],
-                    in0=minus_mean[:, tau : tau + 1],
-                    scalar1=gain[:, tau : tau + 1],
-                    scalar2=ada_offset[:, tau : tau + 1],
-                    op0=ALU.mult,
-                    op1=ALU.add,
-                )
-            for tau in range(PAIR * group, PAIR * group + PAIR):
+                offset[tau] = work.tile([P, 1], F32, name="offset")
                 result[tau] = work.tile([P, CHANNELS], F32, name="result")
                 if tau < TOKEN_TILES // 2:
+                    nc.gpsimd.tensor_scalar(
+                        out=offset[tau][:],
+                        in0=minus_mean[:, tau : tau + 1],
+                        scalar1=gain[:, tau : tau + 1],
+                        scalar2=ada_offset[:, tau : tau + 1],
+                        op0=ALU.mult,
+                        op1=ALU.add,
+                    )
                     nc.gpsimd.tensor_scalar(
                         out=result[tau][:],
                         in0=x_sb[:, tau, :],
                         scalar1=1.0,
-                        scalar2=offset[:, tau : tau + 1],
+                        scalar2=offset[tau][:],
                         op0=ALU.mult,
                         op1=ALU.add,
                     )
                 else:
                     nc.scalar.activation(
+                        out=offset[tau][:],
+                        in_=minus_mean[:, tau : tau + 1],
+                        func=ACT.Identity,
+                        scale=gain[:, tau : tau + 1],
+                        bias=ada_offset[:, tau : tau + 1],
+                    )
+                    nc.scalar.activation(
                         out=result[tau][:],
                         in_=x_sb[:, tau, :],
                         func=ACT.Identity,
-                        bias=offset[:, tau : tau + 1],
+                        bias=offset[tau][:],
                     )
 
         def finish(group):
             for tau in range(PAIR * group, PAIR * group + PAIR):
-                nc.vector.scalar_tensor_tensor(
-                    out=result[tau][:],
-                    in0=projected[tau][:],
-                    scalar=gain[:, tau : tau + 1],
-                    in1=result[tau][:],
-                    op0=ALU.mult,
-                    op1=ALU.add,
-                )
-                nc.sync.dma_start(out=out_rows[output_rows(tau), :], in_=result[tau][:])
+                pieces = 2 if tau == TOKEN_TILES - 1 else 1
+                width = CHANNELS // pieces
+                for piece in range(pieces):
+                    columns = slice(piece * width, (piece + 1) * width)
+                    nc.vector.scalar_tensor_tensor(
+                        out=result[tau][:, columns],
+                        in0=projected[tau][:, columns],
+                        scalar=gain[:, tau : tau + 1],
+                        in1=result[tau][:, columns],
+                        op0=ALU.mult,
+                        op1=ALU.add,
+                    )
+                    nc.sync.dma_start(
+                        out=out_rows[output_rows(tau), columns], in_=result[tau][:, columns]
+                    )
 
         turn_tokens(0)
         quantise_tokens(0)
-        turn_weights(0)
+        prepare_weights(0)
         spread_small_vectors()
-        quantise_weights(0)
-        for pair in range(1, GROUPS):
-            turn_weights(pair)
-            quantise_weights(pair)
+        for block in range(1, W_BLOCKS):
+            prepare_weights(block)
         turn_tokens(1)
         turn_tokens(2)
         quantise_tokens(1)

@@ -20,7 +20,6 @@ PASSES = K // K_PASS
 N_TILE = 512
 N_TILES = CHANNELS // N_TILE
 TOKEN_TILES = TOKENS // P
-W_BLOCKS = CHANNELS // P
 GRID = 32
 WINDOW = 8
 SHIFT = 4
@@ -105,15 +104,15 @@ def tile_swintransformerblock_pb_kernel(
         nc.vector.tensor_copy(out=staying[:, :, WINDOW:stay], in_=window3[:, :, 0 : WINDOW - SHIFT])
         nc.vector.tensor_copy(out=wrapping, in_=window3[:, :, WINDOW - SHIFT : WINDOW])
 
-        w_raw = keep.tile([P, W_BLOCKS, K], BF16)
+        w_raw = keep.tile([P, TOKEN_TILES, K], BF16)
         a_raw = keep.tile([P, TOKEN_TILES, K], BF16)
         x_sb = keep.tile([P, TOKEN_TILES, CHANNELS], BF16)
 
-        def load_tokens(group):
-            blocks = slice(PAIR * group, PAIR * group + PAIR)
+        def load_pair(raw, rows, pair):
+            blocks = slice(PAIR * pair, PAIR * pair + PAIR)
             nc.sync.dma_start(
-                out=a_raw[:, blocks, :],
-                in_=attn_rows[PAIR * P * group : PAIR * P * (group + 1), :].rearrange(
+                out=raw[:, blocks, :],
+                in_=rows[PAIR * P * pair : PAIR * P * (pair + 1), :].rearrange(
                     "(b p) k -> p b k", p=P
                 ),
             )
@@ -126,11 +125,11 @@ def tile_swintransformerblock_pb_kernel(
             for tau in range(PAIR * group, PAIR * group + PAIR):
                 nc.sync.dma_start(out=x_sb[:, tau, :], in_=x_rows[output_rows(tau), :])
 
-        load_tokens(0)
-        for block in range(W_BLOCKS):
-            nc.sync.dma_start(out=w_raw[:, block, :], in_=out_w[block * P : (block + 1) * P, :])
+        load_pair(a_raw, attn_rows, 0)
+        for pair in range(GROUPS):
+            load_pair(w_raw, out_w, pair)
         for group in range(1, GROUPS):
-            load_tokens(group)
+            load_pair(a_raw, attn_rows, group)
         for group in range(GROUPS):
             load_x(group)
 
@@ -143,13 +142,18 @@ def tile_swintransformerblock_pb_kernel(
         w_words = w_grouped[:].bitcast(F32)
         a_grid = a_grouped[:].bitcast(F32).rearrange("p g (i j) u -> p g i j u", j=GRID)
 
-        def prepare_weights(block):
-            rows = slice(block * P, (block + 1) * P)
-            turned = transpose_block(nc, psum_turned, w_raw[:, block, :].bitcast(F32), identity[:])
-            nc.scalar.copy(
-                out=w_words[:, :, rows, :], in_=turned[:].rearrange("p g u c -> p g c u")
-            )
-            quantise(nc, w_grouped, w_codes, w_scales, rows)
+        def turn_weights(pair):
+            for block in range(PAIR * pair, PAIR * pair + PAIR):
+                turned = transpose_block(
+                    nc, psum_turned, w_raw[:, block, :].bitcast(F32), identity[:]
+                )
+                nc.scalar.copy(
+                    out=w_words[:, :, block * P : (block + 1) * P, :],
+                    in_=turned[:].rearrange("p g u c -> p g c u"),
+                )
+
+        def quantise_weights(pair):
+            quantise(nc, w_grouped, w_codes, w_scales, slice(PAIR * P * pair, PAIR * P * (pair + 1)))
 
         def turn_tokens(group):
             grid_rows = slice(WINDOW * group, WINDOW * (group + 1))
@@ -195,57 +199,57 @@ def tile_swintransformerblock_pb_kernel(
             nc.vector.reciprocal(out=inv_ada_gain[:], in_=ada_gain)
 
         sums = const.tile([P, TOKEN_TILES, N_TILES], F32)
+        scaled_sums = const.tile([P, TOKEN_TILES, N_TILES], F32)
         minus_mean = const.tile([P, TOKEN_TILES], F32)
         squares = const.tile([P, TOKEN_TILES], F32)
         std = const.tile([P, TOKEN_TILES], F32)
         gain = const.tile([P, TOKEN_TILES], F32)
-        offset = {}
+        offset = const.tile([P, TOKEN_TILES], F32)
         projected = {}
         result = {}
 
-        def project(group):
-            taus = range(PAIR * group, PAIR * group + PAIR)
-            pair = slice(PAIR * group, PAIR * group + PAIR)
-            acc = {}
-            for n in range(N_TILES):
-                columns = slice(n * N_TILE, (n + 1) * N_TILE)
-                for tau in taus:
-                    tokens = slice(tau * P, (tau + 1) * P)
-                    acc[tau, n] = psum_acc.tile([P, N_TILE], F32, name="acc")
-                    for g in range(PASSES):
-                        nc.tensor.matmul_mx(
-                            out=acc[tau, n][:],
-                            lhsT=a_codes[:, g, tokens].bitcast(FP8X4),
-                            lhsT_scale=a_scales[:, g, tokens],
-                            rhs=w_codes[:, g, columns].bitcast(FP8X4),
-                            rhs_scale=w_scales[:, g, columns],
-                            start=(g == 0),
-                            stop=(g == PASSES - 1),
-                        )
-            if group + 3 < GROUPS:
-                turn_tokens(group + 3)
-            for tau in taus:
-                projected[tau] = work.tile([P, CHANNELS], F32, name="projected")
-            for n in range(N_TILES):
-                columns = slice(n * N_TILE, (n + 1) * N_TILE)
-                for tau in taus:
-                    nc.vector.scalar_tensor_tensor(
-                        out=projected[tau][:, columns],
-                        in0=acc[tau, n][:],
-                        scalar=1.0,
-                        in1=bias_all[:, columns],
-                        op0=ALU.mult,
-                        op1=ALU.add,
-                        accum_out=sums[:, tau, n : n + 1],
+        acc = {}
+
+        def matmuls(group, n):
+            columns = slice(n * N_TILE, (n + 1) * N_TILE)
+            for tau in range(PAIR * group, PAIR * group + PAIR):
+                tokens = slice(tau * P, (tau + 1) * P)
+                acc[tau, n] = psum_acc.tile([P, N_TILE], F32, name="acc")
+                for g in range(PASSES):
+                    nc.tensor.matmul_mx(
+                        out=acc[tau, n][:],
+                        lhsT=a_codes[:, g, tokens].bitcast(FP8X4),
+                        lhsT_scale=a_scales[:, g, tokens],
+                        rhs=w_codes[:, g, columns].bitcast(FP8X4),
+                        rhs_scale=w_scales[:, g, columns],
+                        start=(g == 0),
+                        stop=(g == PASSES - 1),
                     )
-            for tau in taus:
-                nc.gpsimd.tensor_scalar(
-                    out=minus_mean[:, tau : tau + 1],
-                    in0=sums[:, tau, 0:1],
-                    scalar1=sums[:, tau, 1:2],
-                    scalar2=-1.0 / CHANNELS,
-                    op0=ALU.add,
-                    op1=ALU.mult,
+
+        def add_bias(group, n):
+            columns = slice(n * N_TILE, (n + 1) * N_TILE)
+            for tau in range(PAIR * group, PAIR * group + PAIR):
+                if n == 0:
+                    projected[tau] = work.tile([P, CHANNELS], F32, name="projected")
+                nc.vector.scalar_tensor_tensor(
+                    out=projected[tau][:, columns],
+                    in0=acc[tau, n][:],
+                    scalar=1.0,
+                    in1=bias_all[:, columns],
+                    op0=ALU.mult,
+                    op1=ALU.add,
+                    accum_out=sums[:, tau, n : n + 1],
+                )
+
+        def statistics(group):
+            pair = slice(PAIR * group, PAIR * group + PAIR)
+            for tau in range(PAIR * group, PAIR * group + PAIR):
+                nc.scalar.activation(
+                    out=scaled_sums[:, tau, :],
+                    in_=sums[:, tau, :],
+                    func=ACT.Identity,
+                    scale=-1.0 / CHANNELS,
+                    accum_out=minus_mean[:, tau : tau + 1],
                 )
                 deviation_squared = work.tile([P, CHANNELS], BF16, name="deviation_squared")
                 nc.scalar.activation(
@@ -271,38 +275,31 @@ def tile_swintransformerblock_pb_kernel(
             )
             nc.vector.reciprocal(out=gain[:, pair], in_=gain[:, pair])
             for tau in range(PAIR * group, PAIR * group + PAIR):
-                offset[tau] = work.tile([P, 1], F32, name="offset")
+                nc.vector.tensor_scalar(
+                    out=offset[:, tau : tau + 1],
+                    in0=minus_mean[:, tau : tau + 1],
+                    scalar1=gain[:, tau : tau + 1],
+                    scalar2=ada_offset[:, tau : tau + 1],
+                    op0=ALU.mult,
+                    op1=ALU.add,
+                )
+            for tau in range(PAIR * group, PAIR * group + PAIR):
                 result[tau] = work.tile([P, CHANNELS], F32, name="result")
                 if tau < TOKEN_TILES // 2:
-                    nc.gpsimd.tensor_scalar(
-                        out=offset[tau][:],
-                        in0=minus_mean[:, tau : tau + 1],
-                        scalar1=gain[:, tau : tau + 1],
-                        scalar2=ada_offset[:, tau : tau + 1],
-                        op0=ALU.mult,
-                        op1=ALU.add,
-                    )
                     nc.gpsimd.tensor_scalar(
                         out=result[tau][:],
                         in0=x_sb[:, tau, :],
                         scalar1=1.0,
-                        scalar2=offset[tau][:],
+                        scalar2=offset[:, tau : tau + 1],
                         op0=ALU.mult,
                         op1=ALU.add,
                     )
                 else:
                     nc.scalar.activation(
-                        out=offset[tau][:],
-                        in_=minus_mean[:, tau : tau + 1],
-                        func=ACT.Identity,
-                        scale=gain[:, tau : tau + 1],
-                        bias=ada_offset[:, tau : tau + 1],
-                    )
-                    nc.scalar.activation(
                         out=result[tau][:],
                         in_=x_sb[:, tau, :],
                         func=ACT.Identity,
-                        bias=offset[tau][:],
+                        bias=offset[:, tau : tau + 1],
                     )
 
         def finish(group):
@@ -325,19 +322,35 @@ def tile_swintransformerblock_pb_kernel(
 
         turn_tokens(0)
         quantise_tokens(0)
-        prepare_weights(0)
+        turn_weights(0)
         spread_small_vectors()
-        for block in range(1, W_BLOCKS):
-            prepare_weights(block)
+        quantise_weights(0)
+        turn_weights(1)
+        quantise_weights(1)
+        turn_weights(2)
+        matmuls(0, 0)
+        quantise_weights(2)
+        turn_weights(3)
+        add_bias(0, 0)
+        quantise_weights(3)
         turn_tokens(1)
         turn_tokens(2)
         quantise_tokens(1)
-        for step in range(GROUPS + 3):
+        matmuls(0, 1)
+        turn_tokens(3)
+        add_bias(0, 1)
+        statistics(0)
+        quantise_tokens(2)
+        for step in range(1, GROUPS + 3):
             if step < GROUPS:
-                project(step)
+                for n in range(N_TILES):
+                    matmuls(step, n)
+                for n in range(N_TILES):
+                    add_bias(step, n)
+                statistics(step)
             if step + 2 < GROUPS:
                 quantise_tokens(step + 2)
             if step >= 3:
                 finish(step - 3)
-            if 1 <= step <= GROUPS:
+            if step <= GROUPS:
                 shift_residual(step - 1)

from contextlib import ExitStack

import concourse.mybir as mybir
from concourse.masks import make_identity

F32 = mybir.dt.float32
BF16 = mybir.dt.bfloat16
U32 = mybir.dt.uint32
U8 = mybir.dt.uint8
FP8X4 = mybir.dt.float8_e4m3fn_x4
ALU = mybir.AluOpType
ACT = mybir.ActivationFunctionType

P = 128
TOKENS = 1024
CHANNELS = 1024
K = 1024
K_PASS = 4 * P
PASSES = K // K_PASS
N_TILE = 512
N_TILES = CHANNELS // N_TILE
TOKEN_TILES = TOKENS // P
GRID = 32
WINDOW = 8
SHIFT = 4
PAIR = 2
GROUPS = TOKEN_TILES // PAIR
EPS = 1e-5

FLOPS = 2 * TOKENS * CHANNELS * K


def transpose_block(nc, psum, words, order):
    turned = psum.tile([P, PASSES, 2, P], F32, name="turned")
    for g in range(PASSES):
        for u in range(2):
            first = (2 * g + u) * P
            nc.tensor.transpose(turned[:, g, u, :], words[:, first : first + P], order)
    return turned


def quantise(nc, grouped, codes, scales, columns):
    for g in range(PASSES):
        nc.vector.quantize_mx(
            out=codes[:, g, columns].bitcast(FP8X4),
            scales=scales[:, g, columns],
            in_=grouped[:, g, columns, :].rearrange("p c t -> p (c t)"),
        )


def tile_swintransformerblock_pb_kernel(
    tc, o_attn, out_w, out_b, ada1_scale, ada1_shift, x, out
):
    nc = tc.nc
    attn_rows = o_attn.flatten_outer_dims()
    x_rows = x.flatten_outer_dims()
    out_rows = out.flatten_outer_dims()

    with ExitStack() as stack:
        const = stack.enter_context(tc.tile_pool(name="const", bufs=1))
        keep = stack.enter_context(tc.tile_pool(name="keep", bufs=1))
        work = stack.enter_context(tc.tile_pool(name="work", bufs=TOKEN_TILES))
        psum_turned = stack.enter_context(tc.psum_pool(name="psum_turned", bufs=4))
        psum_acc = stack.enter_context(tc.psum_pool(name="psum_acc", bufs=4))
        stack.enter_context(tc.manual_schedule())

        bias_row = const.tile([P, CHANNELS], BF16)
        nc.vector.memset(bias_row[:], 0.0)
        ada_rows = const.tile([P, P], BF16)
        nc.vector.memset(ada_rows[:], 0.0)
        nc.scalar.dma_start(out=bias_row[0:1, :], in_=out_b.unsqueeze(0))
        for first, vector in ((0, ada1_scale), (TOKEN_TILES, ada1_shift)):
            rows = vector.rearrange("o (t p) i -> (o t) (p i)", p=P)
            nc.scalar.dma_start(
                out=ada_rows[first : first + TOKEN_TILES - 1, :], in_=rows[1:TOKEN_TILES, :]
            )
            nc.scalar.dma_start(
                out=ada_rows[first + TOKEN_TILES - 1 : first + TOKEN_TILES, :], in_=rows[0:1, :]
            )

        warm = const.tile([P, 1], F32)
        nc.vector.memset(warm[:], 1.0)
        nc.scalar.activation(out=warm[:], in_=warm[:], func=ACT.Sqrt)
        ones = const.tile([P, P], BF16)
        nc.vector.memset(ones[:], 1.0)

        identity = const.tile([P, P], F32)
        make_identity(nc, identity[:])
        identity_bf16 = const.tile([P, P], BF16)
        nc.vector.tensor_copy(out=identity_bf16[:], in_=identity[:])

        order_left = const.tile([P, P], F32)
        nc.vector.tensor_copy(
            out=order_left[:].rearrange("p (r d c) -> p r d c", r=WINDOW, d=2),
            in_=identity[:].rearrange("p (d r c) -> p r d c", d=2, r=WINDOW),
        )
        stay = 2 * WINDOW - SHIFT
        order_right = const.tile([P, P], F32)
        staying = order_right[:, 0 : WINDOW * stay].rearrange("p (r j) -> p r j", j=stay)
        wrapping = order_right[:, WINDOW * stay : P].rearrange("p (r j) -> p r j", j=SHIFT)
        window2 = identity[:, 0:64].rearrange("p (r c) -> p r c", c=WINDOW)
        window3 = identity[:, 64:128].rearrange("p (r c) -> p r c", c=WINDOW)
        nc.vector.tensor_copy(out=staying[:, :, 0:WINDOW], in_=window2)
        nc.vector.tensor_copy(out=staying[:, :, WINDOW:stay], in_=window3[:, :, 0 : WINDOW - SHIFT])
        nc.vector.tensor_copy(out=wrapping, in_=window3[:, :, WINDOW - SHIFT : WINDOW])

        w_raw = keep.tile([P, TOKEN_TILES, K], BF16)
        a_raw = keep.tile([P, TOKEN_TILES, K], BF16)
        x_sb = keep.tile([P, TOKEN_TILES, CHANNELS], BF16)

        def load_pair(raw, rows, pair):
            blocks = slice(PAIR * pair, PAIR * pair + PAIR)
            nc.sync.dma_start(
                out=raw[:, blocks, :],
                in_=rows[PAIR * P * pair : PAIR * P * (pair + 1), :].rearrange(
                    "(b p) k -> p b k", p=P
                ),
            )

        def output_rows(tau):
            first = ((tau + 1) % TOKEN_TILES) * P
            return slice(first, first + P)

        def load_x(group):
            for tau in range(PAIR * group, PAIR * group + PAIR):
                nc.sync.dma_start(out=x_sb[:, tau, :], in_=x_rows[output_rows(tau), :])

        load_pair(a_raw, attn_rows, 0)
        for pair in range(GROUPS):
            load_pair(w_raw, out_w, pair)
        for group in range(1, GROUPS):
            load_pair(a_raw, attn_rows, group)
        for group in range(GROUPS):
            load_x(group)

        w_grouped = keep.tile([P, PASSES, CHANNELS, 4], BF16, align_bytes=64)
        w_codes = keep.tile([P, PASSES, CHANNELS], U32, align_bytes=64)
        w_scales = keep.tile([P, PASSES, CHANNELS], U8, align_bytes=64)
        a_grouped = keep.tile([P, PASSES, TOKENS, 4], BF16, align_bytes=64)
        a_codes = keep.tile([P, PASSES, TOKENS], U32, align_bytes=64)
        a_scales = keep.tile([P, PASSES, TOKENS], U8, align_bytes=64)
        w_words = w_grouped[:].bitcast(F32)
        a_grid = a_grouped[:].bitcast(F32).rearrange("p g (i j) u -> p g i j u", j=GRID)

        def turn_weights(pair):
            for block in range(PAIR * pair, PAIR * pair + PAIR):
                turned = transpose_block(
                    nc, psum_turned, w_raw[:, block, :].bitcast(F32), identity[:]
                )
                nc.scalar.copy(
                    out=w_words[:, :, block * P : (block + 1) * P, :],
                    in_=turned[:].rearrange("p g u c -> p g c u"),
                )

        def quantise_weights(pair):
            quantise(nc, w_grouped, w_codes, w_scales, slice(PAIR * P * pair, PAIR * P * (pair + 1)))

        def turn_tokens(group):
            grid_rows = slice(WINDOW * group, WINDOW * (group + 1))
            left = transpose_block(
                nc, psum_turned, a_raw[:, PAIR * group, :].bitcast(F32), order_left[:]
            )
            nc.scalar.copy(
                out=a_grid[:, :, grid_rows, SHIFT : SHIFT + 2 * WINDOW, :],
                in_=left[:].rearrange("p g u (r j) -> p g r j u", j=2 * WINDOW),
            )
            right = transpose_block(
                nc, psum_turned, a_raw[:, PAIR * group + 1, :].bitcast(F32), order_right[:]
            )
            nc.scalar.copy(
                out=a_grid[:, :, grid_rows, GRID - stay : GRID, :],
                in_=right[:, :, :, 0 : WINDOW * stay].rearrange("p g u (r j) -> p g r j u", j=stay),
            )
            nc.scalar.copy(
                out=a_grid[:, :, grid_rows, 0:SHIFT, :],
                in_=right[:, :, :, WINDOW * stay : P].rearrange("p g u (r j) -> p g r j u", j=SHIFT),
            )

        def quantise_tokens(group):
            quantise(nc, a_grouped, a_codes, a_scales, slice(PAIR * P * group, PAIR * P * (group + 1)))

        bias_all = const.tile([P, CHANNELS], F32)
        ada = const.tile([P, 2 * TOKEN_TILES], F32)
        ada_gain = ada[:, 0:TOKEN_TILES]
        ada_offset = ada[:, TOKEN_TILES : 2 * TOKEN_TILES]
        inv_ada_gain = const.tile([P, TOKEN_TILES], F32)

        def spread_small_vectors():
            for n in range(N_TILES):
                columns = slice(n * N_TILE, (n + 1) * N_TILE)
                spread = psum_acc.tile([P, N_TILE], F32, name="acc")
                nc.tensor.matmul(
                    out=spread[:], lhsT=ones[:], rhs=bias_row[:, columns], start=True, stop=True
                )
                nc.vector.tensor_copy(out=bias_all[:, columns], in_=spread[:])
            ada_turned = psum_turned.tile([P, P], BF16, name="turned")
            nc.tensor.transpose(ada_turned[:], ada_rows[:], identity_bf16[:])
            nc.vector.tensor_copy(out=ada[:], in_=ada_turned[:, 0 : 2 * TOKEN_TILES])
            nc.vector.reciprocal(out=inv_ada_gain[:], in_=ada_gain)

        sums = const.tile([P, TOKEN_TILES, N_TILES], F32)
        scaled_sums = const.tile([P, TOKEN_TILES, N_TILES], F32)
        minus_mean = const.tile([P, TOKEN_TILES], F32)
        squares = const.tile([P, TOKEN_TILES], F32)
        std = const.tile([P, TOKEN_TILES], F32)
        gain = const.tile([P, TOKEN_TILES], F32)
        offset = const.tile([P, TOKEN_TILES], F32)
        projected = {}
        result = {}

        acc = {}

        def matmuls(group, n):
            columns = slice(n * N_TILE, (n + 1) * N_TILE)
            for tau in range(PAIR * group, PAIR * group + PAIR):
                tokens = slice(tau * P, (tau + 1) * P)
                acc[tau, n] = psum_acc.tile([P, N_TILE], F32, name="acc")
                for g in range(PASSES):
                    nc.tensor.matmul_mx(
                        out=acc[tau, n][:],
                        lhsT=a_codes[:, g, tokens].bitcast(FP8X4),
                        lhsT_scale=a_scales[:, g, tokens],
                        rhs=w_codes[:, g, columns].bitcast(FP8X4),
                        rhs_scale=w_scales[:, g, columns],
                        start=(g == 0),
                        stop=(g == PASSES - 1),
                    )

        def add_bias(group, n):
            columns = slice(n * N_TILE, (n + 1) * N_TILE)
            for tau in range(PAIR * group, PAIR * group + PAIR):
                if n == 0:
                    projected[tau] = work.tile([P, CHANNELS], F32, name="projected")
                nc.vector.scalar_tensor_tensor(
                    out=projected[tau][:, columns],
                    in0=acc[tau, n][:],
                    scalar=1.0,
                    in1=bias_all[:, columns],
                    op0=ALU.mult,
                    op1=ALU.add,
                    accum_out=sums[:, tau, n : n + 1],
                )

        def statistics(group):
            pair = slice(PAIR * group, PAIR * group + PAIR)
            for tau in range(PAIR * group, PAIR * group + PAIR):
                nc.scalar.activation(
                    out=scaled_sums[:, tau, :],
                    in_=sums[:, tau, :],
                    func=ACT.Identity,
                    scale=-1.0 / CHANNELS,
                    accum_out=minus_mean[:, tau : tau + 1],
                )
                deviation_squared = work.tile([P, CHANNELS], BF16, name="deviation_squared")
                nc.scalar.activation(
                    out=deviation_squared[:],
                    in_=projected[tau][:],
                    func=ACT.Square,
                    bias=minus_mean[:, tau : tau + 1],
                    accum_out=squares[:, tau : tau + 1],
                )
            nc.scalar.activation(
                out=std[:, pair], in_=squares[:, pair], func=ACT.Sqrt, scale=1.0 / (CHANNELS - 1)
            )

        def shift_residual(group):
            pair = slice(PAIR * group, PAIR * group + PAIR)
            nc.vector.scalar_tensor_tensor(
                out=gain[:, pair],
                in0=std[:, pair],
                scalar=EPS,
                in1=inv_ada_gain[:, pair],
                op0=ALU.add,
                op1=ALU.mult,
            )
            nc.vector.reciprocal(out=gain[:, pair], in_=gain[:, pair])
            for tau in range(PAIR * group, PAIR * group + PAIR):
                nc.vector.tensor_scalar(
                    out=offset[:, tau : tau + 1],
                    in0=minus_mean[:, tau : tau + 1],
                    scalar1=gain[:, tau : tau + 1],
                    scalar2=ada_offset[:, tau : tau + 1],
                    op0=ALU.mult,
                    op1=ALU.add,
                )
            for tau in range(PAIR * group, PAIR * group + PAIR):
                result[tau] = work.tile([P, CHANNELS], F32, name="result")
                if tau < TOKEN_TILES // 2:
                    nc.gpsimd.tensor_scalar(
                        out=result[tau][:],
                        in0=x_sb[:, tau, :],
                        scalar1=1.0,
                        scalar2=offset[:, tau : tau + 1],
                        op0=ALU.mult,
                        op1=ALU.add,
                    )
                else:
                    nc.scalar.activation(
                        out=result[tau][:],
                        in_=x_sb[:, tau, :],
                        func=ACT.Identity,
                        bias=offset[:, tau : tau + 1],
                    )

        def finish(group):
            for tau in range(PAIR * group, PAIR * group + PAIR):
                pieces = 2 if tau == TOKEN_TILES - 1 else 1
                width = CHANNELS // pieces
                for piece in range(pieces):
                    columns = slice(piece * width, (piece + 1) * width)
                    nc.vector.scalar_tensor_tensor(
                        out=result[tau][:, columns],
                        in0=projected[tau][:, columns],
                        scalar=gain[:, tau : tau + 1],
                        in1=result[tau][:, columns],
                        op0=ALU.mult,
                        op1=ALU.add,
                    )
                    nc.sync.dma_start(
                        out=out_rows[output_rows(tau), columns], in_=result[tau][:, columns]
                    )

        turn_tokens(0)
        quantise_tokens(0)
        turn_weights(0)
        spread_small_vectors()
        quantise_weights(0)
        turn_weights(1)
        quantise_weights(1)
        turn_weights(2)
        matmuls(0, 0)
        quantise_weights(2)
        turn_weights(3)
        add_bias(0, 0)
        quantise_weights(3)
        turn_tokens(1)
        turn_tokens(2)
        quantise_tokens(1)
        matmuls(0, 1)
        turn_tokens(3)
        add_bias(0, 1)
        statistics(0)
        quantise_tokens(2)
        for step in range(1, GROUPS + 3):
            if step < GROUPS:
                for n in range(N_TILES):
                    matmuls(step, n)
                for n in range(N_TILES):
                    add_bias(step, n)
                statistics(step)
            if step + 2 < GROUPS:
                quantise_tokens(step + 2)
            if step >= 3:
                finish(step - 3)
            if step <= GROUPS:
                shift_residual(step - 1)
